import numpy as np
import ml_dtypes


def mxq(x, axis, fmt="e4m3"):
    dtype, down = {"e4m3": (ml_dtypes.float8_e4m3fn, 7), "e5m2": (ml_dtypes.float8_e5m2, 14)}[fmt]
    v = np.moveaxis(np.asarray(x, np.float32).astype(ml_dtypes.bfloat16).astype(np.float64), axis, -1)
    blocks = v.reshape(v.shape[:-1] + (-1, 32))
    amax = np.abs(blocks).max(-1, keepdims=True)
    byte = np.maximum(np.where(amax > 0, np.frexp(amax)[1] - 1 + 127, 0) - down, 1)
    scale = np.exp2(byte - 127.0)
    codes = (blocks / scale).astype(np.float32).astype(dtype).astype(np.float64)
    return np.moveaxis((codes * scale).reshape(v.shape), -1, axis)


WIDE = False


def mx_kscale(k):
    if not WIDE:
        return np.ones(k)
    levels = np.array([10, -10, 5, -5, 0])
    a = np.random.permutation(np.resize(levels, k // 512 * 4)).reshape(k // 512, 4)
    idx = np.arange(k)
    return np.exp2(a[idx // 512, idx % 128 // 32])


BF16 = ml_dtypes.bfloat16


def bf(x):
    return np.asarray(x, np.float32).astype(BF16)


def f64(x):
    return np.asarray(x).astype(np.float64)


B, S, H, NH, NKV, HD = 2, 256, 2048, 16, 4, 128
ROPE_THETA = 10000.0


def rope_tables():
    inv_freq = 1.0 / (ROPE_THETA ** (np.arange(0, HD, 2) / HD))
    pos = np.arange(S)[None, :] + np.random.randint(0, S, (B, 1))
    freqs = pos[:, :, None] * inv_freq[None, None, :]
    emb = np.concatenate([freqs, freqs], axis=-1)
    return np.cos(emb), np.sin(emb)


def rotate_half(x):
    x1, x2 = np.split(x, 2, axis=-1)
    return np.concatenate([-x2, x1], axis=-1)


def setup_inputs():
    s = mx_kscale(H)
    hidden_states = bf(np.random.standard_normal((B, S, H)) * s)
    q_w = bf(np.random.standard_normal((NH * HD, H)) / np.sqrt(H) / s[None, :])
    k_w = bf(np.random.standard_normal((NKV * HD, H)) / np.sqrt(H) / s[None, :])
    v_w = bf(np.random.standard_normal((NKV * HD, H)) / np.sqrt(H) / s[None, :])
    cos, sin = rope_tables()
    return {"hidden_states": hidden_states, "cos": bf(cos), "sin": bf(sin), "q_w": q_w, "k_w": k_w, "v_w": v_w}


def reference(hidden_states, cos, sin, q_w, k_w, v_w):
    b, s, _ = hidden_states.shape
    xq = mxq(f64(hidden_states), 2, "e4m3")
    q = (xq @ mxq(f64(q_w), 1, "e4m3").T).reshape(b, s, NH, HD).transpose(0, 2, 1, 3)
    k = (xq @ mxq(f64(k_w), 1, "e4m3").T).reshape(b, s, NKV, HD).transpose(0, 2, 1, 3)
    v = (xq @ mxq(f64(v_w), 1, "e4m3").T).reshape(b, s, NKV, HD).transpose(0, 2, 1, 3)
    c = f64(cos)[:, None, :, :]
    sn = f64(sin)[:, None, :, :]
    q = q * c + rotate_half(q) * sn
    k = k * c + rotate_half(k) * sn
    return (q, k, v)

@@ -1,0 +1,223 @@
+from contextlib import ExitStack
+
+import concourse.mybir as mybir
+from concourse.masks import make_identity
+
+FLOPS = 2 * 512 * 3072 * 2048
+
+BF16 = mybir.dt.bfloat16
+F32 = mybir.dt.float32
+U32 = mybir.dt.uint32
+U8 = mybir.dt.uint8
+FP8X4 = mybir.dt.float8_e4m3fn_x4
+MULT = mybir.AluOpType.mult
+ADD = mybir.AluOpType.add
+
+P = 128
+H = 2048
+N_UNITS = 14
+VEC_EVAC_UNITS = 3
+GPSIMD_ADD_EVERY = 1
+
+
+def tile_mistralattention_kernel(
+    tc, hidden_states, cos, sin, q_w, k_w, v_w, out_0, out_1, out_2
+):
+    nc = tc.nc
+    with ExitStack() as ctx:
+        src_pool = ctx.enter_context(tc.tile_pool(name="src", bufs=1))
+        const_pool = ctx.enter_context(tc.tile_pool(name="const", bufs=1))
+        grp_pool = ctx.enter_context(tc.tile_pool(name="grp", bufs=3))
+        xq_pool = ctx.enter_context(tc.tile_pool(name="xq", bufs=1))
+        wq_pool = ctx.enter_context(tc.tile_pool(name="wq", bufs=3))
+        tt_pool = ctx.enter_context(tc.tile_pool(name="tt", bufs=4))
+        out_pool = ctx.enter_context(tc.tile_pool(name="outp", bufs=16))
+        tp_pool = ctx.enter_context(tc.psum_pool(name="tp", bufs=4))
+        acc_pool = ctx.enter_context(tc.psum_pool(name="acc", bufs=4))
+        ctx.enter_context(tc.manual_schedule())
+
+        def unit_rows(h):
+            if h < 2:
+                return hidden_states[h].rearrange("(p e) k -> p (e k)", e=2)
+            w = h - 2
+            if w < 8:
+                rows = q_w[256 * w : 256 * w + 256, :]
+            elif w < 10:
+                rows = k_w[256 * (w - 8) : 256 * (w - 8) + 256, :]
+            else:
+                rows = v_w[256 * (w - 10) : 256 * (w - 10) + 256, :]
+            return rows.rearrange("(r p) k -> p r k", p=P)
+
+        def unit_out(h, b):
+            w = h - 2
+            if w < 8:
+                dst = out_0[b, 2 * w : 2 * w + 2]
+            elif w < 10:
+                dst = out_1[b, 2 * (w - 8) : 2 * (w - 8) + 2]
+            else:
+                dst = out_2[b, 2 * (w - 10) : 2 * (w - 10) + 2]
+            return dst.rearrange("h (p e) d -> p h (e d)", e=2)
+
+        ident = const_pool.tile([P, P], F32, name="ident")
+        make_identity(nc, ident[:])
+        cos_sb = const_pool.tile([P, 512], BF16, name="cos_sb")
+        sin_sb = const_pool.tile([P, 512], BF16, name="sin_sb")
+        src = []
+        for h in range(N_UNITS):
+            s_t = src_pool.tile([P, 2 * H], BF16, name="src%d" % h)
+            src.append(s_t)
+            if h < 2:
+                nc.sync.dma_start(out=s_t[:], in_=unit_rows(h))
+            else:
+                nc.sync.dma_start(
+                    out=s_t[:].rearrange("p (r k) -> p r k", r=2), in_=unit_rows(h)
+                )
+            if h == 3:
+                nc.sync.dma_start(
+                    out=cos_sb[:].rearrange("p (b x) -> p b x", b=2),
+                    in_=cos.rearrange("b (p e) d -> p b (e d)", e=2),
+                )
+                nc.sync.dma_start(
+                    out=sin_sb[:].rearrange("p (b x) -> p b x", b=2),
+                    in_=sin.rearrange("b (p e) d -> p b (e d)", e=2),
+                )
+
+        tab = const_pool.tile([P, 2048], F32, name="tab")
+        tab_w = tab[:].rearrange("p (a t h c j) -> p a t h c j", a=2, t=4, h=2, c=2)
+        tab_r = tab[:].rearrange("p (a b q c j) -> p a b q c j", a=2, b=2, q=4, c=2)
+        cos_v = cos_sb[:].rearrange("p (t f j) -> p t f j", t=4, f=2)
+        sin_v = sin_sb[:].rearrange("p (t f j) -> p t f j", t=4, f=2)
+
+        def build_tables():
+            for eng, a, c, view, f, sign in (
+                (nc.vector, 0, 0, cos_v, 0, 1.0),
+                (nc.gpsimd, 0, 1, sin_v, 1, 1.0),
+                (nc.vector, 1, 0, cos_v, 1, 1.0),
+                (nc.gpsimd, 1, 1, sin_v, 0, -1.0),
+            ):
+                eng.tensor_scalar(
+                    out=tab_w[:, a, :, :, c, :],
+                    in0=view[:, :, f, :].unsqueeze(2).to_broadcast([P, 4, 2, 64]),
+                    scalar1=sign,
+                    scalar2=0.0,
+                    op0=MULT,
+                    op1=ADD,
+                )
+
+        grouped = {}
+        codes = {}
+        planes = {}
+
+        def transposes(h):
+            s_f = src[h][:].bitcast(F32)
+            g_t = grp_pool.tile([P, 4096], BF16, name="grp", align_bytes=64)
+            grouped[h] = g_t
+            banks = []
+            for g in range(4):
+                pt = tp_pool.tile([P, 512], F32, name="pt")
+                banks.append(pt)
+                for u in range(2):
+                    for r in range(2):
+                        col = 1024 * r + 256 * g + 128 * u
+                        nc.tensor.transpose(
+                            pt[:, 256 * u + 128 * r : 256 * u + 128 * r + 128],
+                            s_f[:, col : col + 128],
+                            ident[:],
+                        )
+            return banks
+
+        def evacuate(h, banks):
+            g_f = grouped[h][:].bitcast(F32)
+            for g in range(4):
+                dst = g_f[:, 512 * g : 512 * g + 512].rearrange("p (o u) -> p o u", u=2)
+                view = banks[g][:].rearrange("p (u o) -> p o u", u=2)
+                if h < VEC_EVAC_UNITS and g % 2 == 1:
+                    nc.vector.tensor_copy(out=dst, in_=view)
+                else:
+                    nc.scalar.copy(out=dst, in_=view)
+
+        def quantise(h):
+            pool = xq_pool if h < 2 else wq_pool
+            tag = "x%d" % h if h < 2 else "w"
+            c_t = pool.tile([P, 1024], U32, name="codes_" + tag, align_bytes=64)
+            p_t = pool.tile([P, 1024], U8, name="plane_" + tag, align_bytes=64)
+            codes[h] = c_t
+            planes[h] = p_t
+            nc.vector.quantize_mx(
+                out=c_t[:].bitcast(FP8X4), scales=p_t[:], in_=grouped[h][:]
+            )
+
+        def multiply(h):
+            done = []
+            for b in range(2):
+                acc = acc_pool.tile([P, 512], F32, name="acc")
+                for e in range(2):
+                    for g in range(4):
+                        xs = slice(256 * g + 128 * e, 256 * g + 128 * e + 128)
+                        ws = slice(256 * g, 256 * g + 256)
+                        nc.tensor.matmul_mx(
+                            out=acc[:, 256 * e : 256 * e + 256],
+                            lhsT=codes[b][:, xs].bitcast(FP8X4),
+                            lhsT_scale=planes[b][:, xs],
+                            rhs=codes[h][:, ws].bitcast(FP8X4),
+                            rhs_scale=planes[h][:, ws],
+                            start=(g == 0),
+                            stop=(g == 3),
+                        )
+                done.append((h, b, acc))
+            return done
+
+        n_adds = [0]
+
+        def finish(h, b, acc):
+            o_t = out_pool.tile([P, 512], F32, name="o_t")
+            o_v = o_t[:].rearrange("p (h e d) -> p e h d", h=2, e=2)
+            if h - 2 >= 10:
+                nc.scalar.copy(
+                    out=o_v, in_=acc[:].rearrange("p (e h d) -> p e h d", e=2, h=2)
+                )
+            else:
+                acc4 = acc[:].rearrange("p (q f j) -> p q f j", q=4, f=2)
+                t_t = tt_pool.tile([P, 1024], F32, name="t_t")
+                tt4 = t_t[:].rearrange("p (q s j) -> p q s j", q=4, s=4)
+                nc.vector.tensor_tensor(
+                    out=tt4[:, :, 0:4:3, :],
+                    in0=acc4[:, :, 0:1, :].to_broadcast([P, 4, 2, 64]),
+                    in1=tab_r[:, 0, b],
+                    op=MULT,
+                )
+                nc.vector.tensor_tensor(
+                    out=tt4[:, :, 1:3, :],
+                    in0=acc4[:, :, 1:2, :].to_broadcast([P, 4, 2, 64]),
+                    in1=tab_r[:, 1, b],
+                    op=MULT,
+                )
+                eng = nc.gpsimd if n_adds[0] % GPSIMD_ADD_EVERY == 0 else nc.vector
+                n_adds[0] += 1
+                eng.tensor_tensor(
+                    out=o_v,
+                    in0=tt4[:, :, 0:2, :].rearrange("p (e h) f j -> p e h (f j)", e=2),
+                    in1=tt4[:, :, 2:4, :].rearrange("p (e h) f j -> p e h (f j)", e=2),
+                    op=ADD,
+                )
+            nc.sync.dma_start(
+                out=unit_out(h, b), in_=o_t[:].rearrange("p (h x) -> p h x", h=2)
+            )
+
+        pending = []
+        for h in range(N_UNITS + 1):
+            if h < N_UNITS:
+                banks = transposes(h)
+                if h >= 1:
+                    quantise(h - 1)
+                evacuate(h, banks)
+                if h == 3:
+                    build_tables()
+            else:
+                quantise(h - 1)
+            if h >= 3:
+                for item in pending:
+                    finish(*item)
+                pending = multiply(h - 1)
+        for item in pending:
+            finish(*item)

@@ -14,10 +14,10 @@ MULT = mybir.AluOpType.mult
 ADD = mybir.AluOpType.add
 
 P = 128
-H = 2048
-N_UNITS = 14
-VEC_EVAC_UNITS = 3
-GPSIMD_ADD_EVERY = 1
+LOAD_ORDER = (0, 2, 1, 3, 4, 5, 6, 7, 8, 9, 10, 11, 12, 13)
+HALVED = (0, 1, 2, 3)
+VECTOR_ADDS = (2, 3, 11)
+FIRST_V_UNIT = 12
 
 
 def tile_mistralattention_kernel(
@@ -30,15 +30,15 @@ def tile_mistralattention_kernel(
         grp_pool = ctx.enter_context(tc.tile_pool(name="grp", bufs=3))
         xq_pool = ctx.enter_context(tc.tile_pool(name="xq", bufs=1))
         wq_pool = ctx.enter_context(tc.tile_pool(name="wq", bufs=3))
-        tt_pool = ctx.enter_context(tc.tile_pool(name="tt", bufs=4))
-        out_pool = ctx.enter_context(tc.tile_pool(name="outp", bufs=16))
+        tt_pool = ctx.enter_context(tc.tile_pool(name="tt", bufs=3))
+        out_pool = ctx.enter_context(tc.tile_pool(name="outp", bufs=7))
         tp_pool = ctx.enter_context(tc.psum_pool(name="tp", bufs=4))
         acc_pool = ctx.enter_context(tc.psum_pool(name="acc", bufs=4))
         ctx.enter_context(tc.manual_schedule())
 
         def unit_rows(h):
             if h < 2:
-                return hidden_states[h].rearrange("(p e) k -> p (e k)", e=2)
+                return hidden_states[h].rearrange("(p e) k -> p e k", e=2)
             w = h - 2
             if w < 8:
                 rows = q_w[256 * w : 256 * w + 256, :]
@@ -62,16 +62,22 @@ def tile_mistralattention_kernel(
         make_identity(nc, ident[:])
         cos_sb = const_pool.tile([P, 512], BF16, name="cos_sb")
         sin_sb = const_pool.tile([P, 512], BF16, name="sin_sb")
-        src = []
-        for h in range(N_UNITS):
-            s_t = src_pool.tile([P, 2 * H], BF16, name="src%d" % h)
-            src.append(s_t)
-            if h < 2:
-                nc.sync.dma_start(out=s_t[:], in_=unit_rows(h))
+
+        src = {}
+        for h in LOAD_ORDER:
+            rows = unit_rows(h)
+            if h in HALVED:
+                for i in range(2):
+                    s_t = src_pool.tile([P, 2048], BF16, name="src%d_%d" % (h, i))
+                    src[(h, i)] = s_t
+                    nc.sync.dma_start(
+                        out=s_t[:].rearrange("p (r k) -> p r k", r=2),
+                        in_=rows[:, :, 1024 * i : 1024 * i + 1024],
+                    )
             else:
-                nc.sync.dma_start(
-                    out=s_t[:].rearrange("p (r k) -> p r k", r=2), in_=unit_rows(h)
-                )
+                s_t = src_pool.tile([P, 4096], BF16, name="src%d" % h)
+                src[(h, 0)] = s_t
+                nc.sync.dma_start(out=s_t[:].rearrange("p (r k) -> p r k", r=2), in_=rows)
             if h == 3:
                 nc.sync.dma_start(
                     out=cos_sb[:].rearrange("p (b x) -> p b x", b=2),
@@ -81,6 +87,15 @@ def tile_mistralattention_kernel(
                     out=sin_sb[:].rearrange("p (b x) -> p b x", b=2),
                     in_=sin.rearrange("b (p e) d -> p b (e d)", e=2),
                 )
+
+        def src_words(h, g, u, r):
+            if h in HALVED:
+                s_f = src[(h, g // 2)][:].bitcast(F32)
+                col = 512 * r + 256 * (g % 2) + 128 * u
+            else:
+                s_f = src[(h, 0)][:].bitcast(F32)
+                col = 1024 * r + 256 * g + 128 * u
+            return s_f[:, col : col + 128]
 
         tab = const_pool.tile([P, 2048], F32, name="tab")
         tab_w = tab[:].rearrange("p (a t h c j) -> p a t h c j", a=2, t=4, h=2, c=2)
@@ -107,50 +122,58 @@ def tile_mistralattention_kernel(
         grouped = {}
         codes = {}
         planes = {}
+        banks = {}
+        sums = {}
 
-        def transposes(h):
-            s_f = src[h][:].bitcast(F32)
-            g_t = grp_pool.tile([P, 4096], BF16, name="grp", align_bytes=64)
-            grouped[h] = g_t
-            banks = []
-            for g in range(4):
+        def transposes(h, gs):
+            if h not in grouped:
+                grouped[h] = grp_pool.tile([P, 4096], BF16, name="grp", align_bytes=64)
+            for g in gs:
                 pt = tp_pool.tile([P, 512], F32, name="pt")
-                banks.append(pt)
+                banks[(h, g)] = pt
                 for u in range(2):
                     for r in range(2):
-                        col = 1024 * r + 256 * g + 128 * u
                         nc.tensor.transpose(
                             pt[:, 256 * u + 128 * r : 256 * u + 128 * r + 128],
-                            s_f[:, col : col + 128],
+                            src_words(h, g, u, r),
                             ident[:],
                         )
-            return banks
 
-        def evacuate(h, banks):
+        def evacuate(h, gs, vector_gs):
             g_f = grouped[h][:].bitcast(F32)
-            for g in range(4):
+            for g in gs:
                 dst = g_f[:, 512 * g : 512 * g + 512].rearrange("p (o u) -> p o u", u=2)
-                view = banks[g][:].rearrange("p (u o) -> p o u", u=2)
-                if h < VEC_EVAC_UNITS and g % 2 == 1:
+                view = banks[(h, g)][:].rearrange("p (u o) -> p o u", u=2)
+                if g in vector_gs:
                     nc.vector.tensor_copy(out=dst, in_=view)
                 else:
                     nc.scalar.copy(out=dst, in_=view)
 
-        def quantise(h):
-            pool = xq_pool if h < 2 else wq_pool
-            tag = "x%d" % h if h < 2 else "w"
-            c_t = pool.tile([P, 1024], U32, name="codes_" + tag, align_bytes=64)
-            p_t = pool.tile([P, 1024], U8, name="plane_" + tag, align_bytes=64)
-            codes[h] = c_t
-            planes[h] = p_t
-            nc.vector.quantize_mx(
-                out=c_t[:].bitcast(FP8X4), scales=p_t[:], in_=grouped[h][:]
-            )
+        def quantise(h, parts):
+            if h not in codes:
+                pool = xq_pool if h < 2 else wq_pool
+                tag = "x%d" % h if h < 2 else "w"
+                codes[h] = pool.tile([P, 1024], U32, name="codes_" + tag, align_bytes=64)
+                planes[h] = pool.tile([P, 1024], U8, name="plane_" + tag, align_bytes=64)
+            for lo, hi in parts:
+                nc.vector.quantize_mx(
+                    out=codes[h][:, lo:hi].bitcast(FP8X4),
+                    scales=planes[h][:, lo:hi],
+                    in_=grouped[h][:, 4 * lo : 4 * hi],
+                )
 
-        def multiply(h):
-            done = []
-            for b in range(2):
+        WHOLE = ((0, 1024),)
+
+        def head_half(h, i):
+            gs = (2 * i, 2 * i + 1)
+            transposes(h, gs)
+            evacuate(h, gs, (2 * i + 1,))
+            quantise(h, ((512 * i, 512 * i + 512),))
+
+        def multiply(h, bs):
+            for b in bs:
                 acc = acc_pool.tile([P, 512], F32, name="acc")
+                sums[(h, b)] = acc
                 for e in range(2):
                     for g in range(4):
                         xs = slice(256 * g + 128 * e, 256 * g + 128 * e + 128)
@@ -164,60 +187,88 @@ def tile_mistralattention_kernel(
                             start=(g == 0),
                             stop=(g == 3),
                         )
-                done.append((h, b, acc))
-            return done
 
-        n_adds = [0]
+        results = {}
 
-        def finish(h, b, acc):
-            o_t = out_pool.tile([P, 512], F32, name="o_t")
-            o_v = o_t[:].rearrange("p (h e d) -> p e h d", h=2, e=2)
-            if h - 2 >= 10:
-                nc.scalar.copy(
-                    out=o_v, in_=acc[:].rearrange("p (e h d) -> p e h d", e=2, h=2)
-                )
-            else:
-                acc4 = acc[:].rearrange("p (q f j) -> p q f j", q=4, f=2)
-                t_t = tt_pool.tile([P, 1024], F32, name="t_t")
-                tt4 = t_t[:].rearrange("p (q s j) -> p q s j", q=4, s=4)
+        def store(h):
+            o_b = results[h][:].rearrange("p (h b x) -> p h b x", h=2, b=2)
+            for b in range(2):
+                nc.sync.dma_start(out=unit_out(h, b), in_=o_b[:, :, b, :])
+
+        def finish(h):
+            o_t = out_pool.tile([P, 1024], F32, name="o_t")
+            results[h] = o_t
+            o_v = o_t[:].rearrange("p (h t d) -> p t h d", h=2, t=4)
+            if h >= FIRST_V_UNIT:
+                for b in range(2):
+                    nc.scalar.copy(
+                        out=o_v[:, 2 * b : 2 * b + 2],
+                        in_=sums[(h, b)][:].rearrange("p (e h d) -> p e h d", e=2, h=2),
+                    )
+                return
+            t_t = tt_pool.tile([P, 2048], F32, name="t_t")
+            tt5 = t_t[:].rearrange("p (b q s j) -> p b q s j", b=2, q=4, s=4)
+            for b in range(2):
+                acc4 = sums[(h, b)][:].rearrange("p (q f j) -> p q f j", q=4, f=2)
                 nc.vector.tensor_tensor(
-                    out=tt4[:, :, 0:4:3, :],
+                    out=tt5[:, b, :, 0:4:3, :],
                     in0=acc4[:, :, 0:1, :].to_broadcast([P, 4, 2, 64]),
                     in1=tab_r[:, 0, b],
                     op=MULT,
                 )
                 nc.vector.tensor_tensor(
-                    out=tt4[:, :, 1:3, :],
+                    out=tt5[:, b, :, 1:3, :],
                     in0=acc4[:, :, 1:2, :].to_broadcast([P, 4, 2, 64]),
                     in1=tab_r[:, 1, b],
                     op=MULT,
                 )
-                eng = nc.gpsimd if n_adds[0] % GPSIMD_ADD_EVERY == 0 else nc.vector
-                n_adds[0] += 1
-                eng.tensor_tensor(
-                    out=o_v,
-                    in0=tt4[:, :, 0:2, :].rearrange("p (e h) f j -> p e h (f j)", e=2),
-                    in1=tt4[:, :, 2:4, :].rearrange("p (e h) f j -> p e h (f j)", e=2),
-                    op=ADD,
-                )
-            nc.sync.dma_start(
-                out=unit_out(h, b), in_=o_t[:].rearrange("p (h x) -> p h x", h=2)
+            tt_u = t_t[:].rearrange("p (t h s j) -> p t h s j", t=4, h=2, s=4)
+            eng = nc.vector if h in VECTOR_ADDS else nc.gpsimd
+            eng.tensor_tensor(
+                out=o_v,
+                in0=tt_u[:, :, :, 0:2, :].rearrange("p t h f j -> p t h (f j)"),
+                in1=tt_u[:, :, :, 2:4, :].rearrange("p t h f j -> p t h (f j)"),
+                op=ADD,
             )
 
-        pending = []
-        for h in range(N_UNITS + 1):
-            if h < N_UNITS:
-                banks = transposes(h)
-                if h >= 1:
-                    quantise(h - 1)
-                evacuate(h, banks)
-                if h == 3:
-                    build_tables()
-            else:
-                quantise(h - 1)
-            if h >= 3:
-                for item in pending:
-                    finish(*item)
-                pending = multiply(h - 1)
-        for item in pending:
-            finish(*item)
+        ALL = (0, 1, 2, 3)
+
+        for h in (0, 2, 1):
+            head_half(h, 0)
+            head_half(h, 1)
+        multiply(2, (0,))
+        transposes(3, ALL)
+        evacuate(3, ALL, (1,))
+        build_tables()
+        quantise(3, ((0, 512), (512, 1024)))
+        multiply(2, (1,))
+        transposes(4, ALL)
+        evacuate(4, ALL, ())
+        finish(2)
+        store(2)
+        multiply(3, (0, 1))
+        transposes(5, ALL)
+        evacuate(5, ALL, ())
+        quantise(4, WHOLE)
+        transposes(6, ALL)
+        evacuate(6, ALL, ())
+        finish(3)
+        store(3)
+        quantise(5, WHOLE)
+        multiply(4, (0, 1))
+        for m in range(5, 14):
+            if m + 2 <= 13:
+                transposes(m + 2, ALL)
+                evacuate(m + 2, ALL, ())
+            if m == 12:
+                quantise(13, WHOLE)
+            finish(m - 1)
+            if m - 1 != 11:
+                store(m - 1)
+            if m - 1 == 12:
+                store(11)
+            if m + 1 <= 12:
+                quantise(m + 1, WHOLE)
+            multiply(m, (0, 1))
+        finish(13)
+        store(13)

@@ -18,6 +18,8 @@ LOAD_ORDER = (0, 2, 1, 3, 4, 5, 6, 7, 8, 9, 10, 11, 12, 13)
 HALVED = (0, 1, 2, 3)
 VECTOR_ADDS = (2, 3, 11)
 FIRST_V_UNIT = 12
+WARM_FIRST = 7
+WARM_BETWEEN = 2
 
 
 def tile_mistralattention_kernel(
@@ -233,9 +235,21 @@ def tile_mistralattention_kernel(
 
         ALL = (0, 1, 2, 3)
 
-        for h in (0, 2, 1):
-            head_half(h, 0)
-            head_half(h, 1)
+        zeros = const_pool.tile([P, 512], BF16, name="zeros")
+        nc.vector.memset(zeros[:], 0.0)
+        warm = acc_pool.tile([P, 512], F32, name="acc")
+
+        def keep_warm(n):
+            for i in range(n):
+                nc.tensor.matmul(
+                    out=warm[:], lhsT=zeros[:, 0:P], rhs=zeros[:], start=True, stop=True
+                )
+
+        keep_warm(WARM_FIRST)
+        for h, i in ((0, 0), (0, 1), (2, 0), (2, 1), (1, 0)):
+            head_half(h, i)
+            keep_warm(WARM_BETWEEN)
+        head_half(1, 1)
         multiply(2, (0,))
         transposes(3, ALL)
         evacuate(3, ALL, (1,))

@@ -18,8 +18,7 @@ LOAD_ORDER = (0, 2, 1, 3, 4, 5, 6, 7, 8, 9, 10, 11, 12, 13)
 HALVED = (0, 1, 2, 3)
 VECTOR_ADDS = (2, 3, 11)
 FIRST_V_UNIT = 12
-WARM_FIRST = 7
-WARM_BETWEEN = 2
+X_PAD = 48
 
 
 def tile_mistralattention_kernel(
@@ -129,7 +128,7 @@ def tile_mistralattention_kernel(
 
         def transposes(h, gs):
             if h not in grouped:
-                grouped[h] = grp_pool.tile([P, 4096], BF16, name="grp", align_bytes=64)
+                grouped[h] = grp_pool.tile([P, 4096], BF16, name="grp", align_bytes=256)
             for g in gs:
                 pt = tp_pool.tile([P, 512], F32, name="pt")
                 banks[(h, g)] = pt
@@ -151,12 +150,23 @@ def tile_mistralattention_kernel(
                 else:
                     nc.scalar.copy(out=dst, in_=view)
 
+        def quantise_x(h, i):
+            if h not in codes:
+                codes[h] = xq_pool.tile(
+                    [P, X_PAD + 1024], U32, name="codes_x%d" % h, align_bytes=256
+                )
+                planes[h] = xq_pool.tile([P, 2048], U8, name="plane_x%d" % h, align_bytes=256)
+            for s in range(4 * i, 4 * i + 4):
+                nc.vector.quantize_mx(
+                    out=codes[h][:, X_PAD + 128 * s : X_PAD + 128 * s + 128].bitcast(FP8X4),
+                    scales=planes[h][:, 256 * s : 256 * s + 128],
+                    in_=grouped[h][:, 512 * s : 512 * s + 512],
+                )
+
         def quantise(h, parts):
             if h not in codes:
-                pool = xq_pool if h < 2 else wq_pool
-                tag = "x%d" % h if h < 2 else "w"
-                codes[h] = pool.tile([P, 1024], U32, name="codes_" + tag, align_bytes=64)
-                planes[h] = pool.tile([P, 1024], U8, name="plane_" + tag, align_bytes=64)
+                codes[h] = wq_pool.tile([P, 1024], U32, name="codes_w", align_bytes=256)
+                planes[h] = wq_pool.tile([P, 1024], U8, name="plane_w", align_bytes=256)
             for lo, hi in parts:
                 nc.vector.quantize_mx(
                     out=codes[h][:, lo:hi].bitcast(FP8X4),
@@ -170,7 +180,10 @@ def tile_mistralattention_kernel(
             gs = (2 * i, 2 * i + 1)
             transposes(h, gs)
             evacuate(h, gs, (2 * i + 1,))
-            quantise(h, ((512 * i, 512 * i + 512),))
+            if h < 2:
+                quantise_x(h, i)
+            else:
+                quantise(h, ((512 * i, 512 * i + 512),))
 
         def multiply(h, bs):
             for b in bs:
@@ -178,12 +191,14 @@ def tile_mistralattention_kernel(
                 sums[(h, b)] = acc
                 for e in range(2):
                     for g in range(4):
-                        xs = slice(256 * g + 128 * e, 256 * g + 128 * e + 128)
+                        s = 2 * g + e
                         ws = slice(256 * g, 256 * g + 256)
                         nc.tensor.matmul_mx(
                             out=acc[:, 256 * e : 256 * e + 256],
-                            lhsT=codes[b][:, xs].bitcast(FP8X4),
-                            lhsT_scale=planes[b][:, xs],
+                            lhsT=codes[b][
+                                :, X_PAD + 128 * s : X_PAD + 128 * s + 128
+                            ].bitcast(FP8X4),
+                            lhsT_scale=planes[b][:, 256 * s : 256 * s + 128],
                             rhs=codes[h][:, ws].bitcast(FP8X4),
                             rhs_scale=planes[h][:, ws],
                             start=(g == 0),
@@ -235,21 +250,9 @@ def tile_mistralattention_kernel(
 
         ALL = (0, 1, 2, 3)
 
-        zeros = const_pool.tile([P, 512], BF16, name="zeros")
-        nc.vector.memset(zeros[:], 0.0)
-        warm = acc_pool.tile([P, 512], F32, name="acc")
-
-        def keep_warm(n):
-            for i in range(n):
-                nc.tensor.matmul(
-                    out=warm[:], lhsT=zeros[:, 0:P], rhs=zeros[:], start=True, stop=True
-                )
-
-        keep_warm(WARM_FIRST)
-        for h, i in ((0, 0), (0, 1), (2, 0), (2, 1), (1, 0)):
-            head_half(h, i)
-            keep_warm(WARM_BETWEEN)
-        head_half(1, 1)
+        for h in (0, 2, 1):
+            head_half(h, 0)
+            head_half(h, 1)
         multiply(2, (0,))
         transposes(3, ALL)
         evacuate(3, ALL, (1,))

@@ -18,7 +18,6 @@ LOAD_ORDER = (0, 2, 1, 3, 4, 5, 6, 7, 8, 9, 10, 11, 12, 13)
 HALVED = (0, 1, 2, 3)
 VECTOR_ADDS = (2, 3, 11)
 FIRST_V_UNIT = 12
-X_PAD = 48
 
 
 def tile_mistralattention_kernel(
@@ -128,7 +127,7 @@ def tile_mistralattention_kernel(
 
         def transposes(h, gs):
             if h not in grouped:
-                grouped[h] = grp_pool.tile([P, 4096], BF16, name="grp", align_bytes=256)
+                grouped[h] = grp_pool.tile([P, 4096], BF16, name="grp", align_bytes=64)
             for g in gs:
                 pt = tp_pool.tile([P, 512], F32, name="pt")
                 banks[(h, g)] = pt
@@ -150,23 +149,12 @@ def tile_mistralattention_kernel(
                 else:
                     nc.scalar.copy(out=dst, in_=view)
 
-        def quantise_x(h, i):
-            if h not in codes:
-                codes[h] = xq_pool.tile(
-                    [P, X_PAD + 1024], U32, name="codes_x%d" % h, align_bytes=256
-                )
-                planes[h] = xq_pool.tile([P, 2048], U8, name="plane_x%d" % h, align_bytes=256)
-            for s in range(4 * i, 4 * i + 4):
-                nc.vector.quantize_mx(
-                    out=codes[h][:, X_PAD + 128 * s : X_PAD + 128 * s + 128].bitcast(FP8X4),
-                    scales=planes[h][:, 256 * s : 256 * s + 128],
-                    in_=grouped[h][:, 512 * s : 512 * s + 512],
-                )
-
         def quantise(h, parts):
             if h not in codes:
-                codes[h] = wq_pool.tile([P, 1024], U32, name="codes_w", align_bytes=256)
-                planes[h] = wq_pool.tile([P, 1024], U8, name="plane_w", align_bytes=256)
+                pool = xq_pool if h < 2 else wq_pool
+                tag = "x%d" % h if h < 2 else "w"
+                codes[h] = pool.tile([P, 1024], U32, name="codes_" + tag, align_bytes=64)
+                planes[h] = pool.tile([P, 1024], U8, name="plane_" + tag, align_bytes=64)
             for lo, hi in parts:
                 nc.vector.quantize_mx(
                     out=codes[h][:, lo:hi].bitcast(FP8X4),
@@ -180,10 +168,7 @@ def tile_mistralattention_kernel(
             gs = (2 * i, 2 * i + 1)
             transposes(h, gs)
             evacuate(h, gs, (2 * i + 1,))
-            if h < 2:
-                quantise_x(h, i)
-            else:
-                quantise(h, ((512 * i, 512 * i + 512),))
+            quantise(h, ((512 * i, 512 * i + 512),))
 
         def multiply(h, bs):
             for b in bs:
@@ -191,14 +176,12 @@ def tile_mistralattention_kernel(
                 sums[(h, b)] = acc
                 for e in range(2):
                     for g in range(4):
-                        s = 2 * g + e
+                        xs = slice(256 * g + 128 * e, 256 * g + 128 * e + 128)
                         ws = slice(256 * g, 256 * g + 256)
                         nc.tensor.matmul_mx(
                             out=acc[:, 256 * e : 256 * e + 256],
-                            lhsT=codes[b][
-                                :, X_PAD + 128 * s : X_PAD + 128 * s + 128
-                            ].bitcast(FP8X4),
-                            lhsT_scale=planes[b][:, 256 * s : 256 * s + 128],
+                            lhsT=codes[b][:, xs].bitcast(FP8X4),
+                            lhsT_scale=planes[b][:, xs],
                             rhs=codes[h][:, ws].bitcast(FP8X4),
                             rhs_scale=planes[h][:, ws],
                             start=(g == 0),
@@ -275,8 +258,8 @@ def tile_mistralattention_kernel(
         multiply(4, (0, 1))
         for m in range(5, 14):
             if m + 2 <= 13:
-                transposes(m + 2, ALL)
-                evacuate(m + 2, ALL, ())
+                transposes(m + 2, (0, 1))
+                evacuate(m + 2, (0, 1), ())
             if m == 12:
                 quantise(13, WHOLE)
             finish(m - 1)
@@ -286,6 +269,10 @@ def tile_mistralattention_kernel(
                 store(11)
             if m + 1 <= 12:
                 quantise(m + 1, WHOLE)
-            multiply(m, (0, 1))
+            multiply(m, (0,))
+            if m + 2 <= 13:
+                transposes(m + 2, (2, 3))
+                evacuate(m + 2, (2, 3), ())
+            multiply(m, (1,))
         finish(13)
         store(13)

@@ -16,7 +16,7 @@ ADD = mybir.AluOpType.add
 P = 128
 LOAD_ORDER = (0, 2, 1, 3, 4, 5, 6, 7, 8, 9, 10, 11, 12, 13)
 HALVED = (0, 1, 2, 3)
-VECTOR_ADDS = (2, 3, 11)
+VECTOR_ADDS = (2, 11)
 FIRST_V_UNIT = 12
 
 
@@ -195,34 +195,40 @@ def tile_mistralattention_kernel(
             for b in range(2):
                 nc.sync.dma_start(out=unit_out(h, b), in_=o_b[:, :, b, :])
 
-        def finish(h):
-            o_t = out_pool.tile([P, 1024], F32, name="o_t")
-            results[h] = o_t
-            o_v = o_t[:].rearrange("p (h t d) -> p t h d", h=2, t=4)
+        terms = {}
+
+        def products(h, b):
+            if h not in results:
+                results[h] = out_pool.tile([P, 1024], F32, name="o_t")
             if h >= FIRST_V_UNIT:
-                for b in range(2):
-                    nc.scalar.copy(
-                        out=o_v[:, 2 * b : 2 * b + 2],
-                        in_=sums[(h, b)][:].rearrange("p (e h d) -> p e h d", e=2, h=2),
-                    )
+                o_v = results[h][:].rearrange("p (h t d) -> p t h d", h=2, t=4)
+                nc.scalar.copy(
+                    out=o_v[:, 2 * b : 2 * b + 2],
+                    in_=sums[(h, b)][:].rearrange("p (e h d) -> p e h d", e=2, h=2),
+                )
                 return
-            t_t = tt_pool.tile([P, 2048], F32, name="t_t")
-            tt5 = t_t[:].rearrange("p (b q s j) -> p b q s j", b=2, q=4, s=4)
-            for b in range(2):
-                acc4 = sums[(h, b)][:].rearrange("p (q f j) -> p q f j", q=4, f=2)
-                nc.vector.tensor_tensor(
-                    out=tt5[:, b, :, 0:4:3, :],
-                    in0=acc4[:, :, 0:1, :].to_broadcast([P, 4, 2, 64]),
-                    in1=tab_r[:, 0, b],
-                    op=MULT,
-                )
-                nc.vector.tensor_tensor(
-                    out=tt5[:, b, :, 1:3, :],
-                    in0=acc4[:, :, 1:2, :].to_broadcast([P, 4, 2, 64]),
-                    in1=tab_r[:, 1, b],
-                    op=MULT,
-                )
-            tt_u = t_t[:].rearrange("p (t h s j) -> p t h s j", t=4, h=2, s=4)
+            if h not in terms:
+                terms[h] = tt_pool.tile([P, 2048], F32, name="t_t")
+            tt5 = terms[h][:].rearrange("p (b q s j) -> p b q s j", b=2, q=4, s=4)
+            acc4 = sums[(h, b)][:].rearrange("p (q f j) -> p q f j", q=4, f=2)
+            nc.vector.tensor_tensor(
+                out=tt5[:, b, :, 0:4:3, :],
+                in0=acc4[:, :, 0:1, :].to_broadcast([P, 4, 2, 64]),
+                in1=tab_r[:, 0, b],
+                op=MULT,
+            )
+            nc.vector.tensor_tensor(
+                out=tt5[:, b, :, 1:3, :],
+                in0=acc4[:, :, 1:2, :].to_broadcast([P, 4, 2, 64]),
+                in1=tab_r[:, 1, b],
+                op=MULT,
+            )
+
+        def combine(h):
+            if h >= FIRST_V_UNIT:
+                return
+            o_v = results[h][:].rearrange("p (h t d) -> p t h d", h=2, t=4)
+            tt_u = terms[h][:].rearrange("p (t h s j) -> p t h s j", t=4, h=2, s=4)
             eng = nc.vector if h in VECTOR_ADDS else nc.gpsimd
             eng.tensor_tensor(
                 out=o_v,
@@ -231,31 +237,45 @@ def tile_mistralattention_kernel(
                 op=ADD,
             )
 
+        def finish(h):
+            products(h, 0)
+            products(h, 1)
+            combine(h)
+
         ALL = (0, 1, 2, 3)
 
         for h in (0, 2, 1):
             head_half(h, 0)
             head_half(h, 1)
         multiply(2, (0,))
-        transposes(3, ALL)
-        evacuate(3, ALL, (1,))
+        transposes(3, (0, 1))
+        evacuate(3, (0, 1), (1,))
         build_tables()
-        quantise(3, ((0, 512), (512, 1024)))
+        quantise(3, ((0, 512),))
         multiply(2, (1,))
+        transposes(3, (2, 3))
+        evacuate(3, (2, 3), ())
+        products(2, 0)
+        quantise(3, ((512, 1024),))
         transposes(4, ALL)
         evacuate(4, ALL, ())
-        finish(2)
+        products(2, 1)
+        combine(2)
         store(2)
-        multiply(3, (0, 1))
+        multiply(3, (0,))
         transposes(5, ALL)
         evacuate(5, ALL, ())
         quantise(4, WHOLE)
-        transposes(6, ALL)
-        evacuate(6, ALL, ())
+        multiply(3, (1,))
+        transposes(6, (0, 1))
+        evacuate(6, (0, 1), ())
         finish(3)
         store(3)
         quantise(5, WHOLE)
-        multiply(4, (0, 1))
+        multiply(4, (0,))
+        transposes(6, (2, 3))
+        evacuate(6, (2, 3), ())
+        multiply(4, (1,))
         for m in range(5, 14):
             if m + 2 <= 13:
                 transposes(m + 2, (0, 1))

@@ -172,9 +172,14 @@ def tile_mistralattention_kernel(
 
         def multiply(h, bs):
             for b in bs:
-                acc = acc_pool.tile([P, 512], F32, name="acc")
-                sums[(h, b)] = acc
-                for e in range(2):
+                multiply_groups(h, b, (0, 1))
+
+        def multiply_groups(h, b, es):
+            if True:
+                if (h, b) not in sums:
+                    sums[(h, b)] = acc_pool.tile([P, 512], F32, name="acc")
+                acc = sums[(h, b)]
+                for e in es:
                     for g in range(4):
                         xs = slice(256 * g + 128 * e, 256 * g + 128 * e + 128)
                         ws = slice(256 * g, 256 * g + 256)
@@ -278,8 +283,8 @@ def tile_mistralattention_kernel(
         multiply(4, (1,))
         for m in range(5, 14):
             if m + 2 <= 13:
-                transposes(m + 2, (0, 1))
-                evacuate(m + 2, (0, 1), ())
+                transposes(m + 2, (0,))
+                evacuate(m + 2, (0,), ())
             if m == 12:
                 quantise(13, WHOLE)
             finish(m - 1)
@@ -289,10 +294,11 @@ def tile_mistralattention_kernel(
                 store(11)
             if m + 1 <= 12:
                 quantise(m + 1, WHOLE)
-            multiply(m, (0,))
-            if m + 2 <= 13:
-                transposes(m + 2, (2, 3))
-                evacuate(m + 2, (2, 3), ())
-            multiply(m, (1,))
+            multiply_groups(m, 0, (0,))
+            for i in (1, 2, 3):
+                if m + 2 <= 13:
+                    transposes(m + 2, (i,))
+                    evacuate(m + 2, (i,), ())
+                multiply_groups(m, i // 2, (i % 2,))
         finish(13)
         store(13)

@@ -16,7 +16,7 @@ ADD = mybir.AluOpType.add
 P = 128
 LOAD_ORDER = (0, 2, 1, 3, 4, 5, 6, 7, 8, 9, 10, 11, 12, 13)
 HALVED = (0, 1, 2, 3)
-VECTOR_ADDS = (2, 11)
+VECTOR_ADDS = (2, 3, 11)
 FIRST_V_UNIT = 12
 
 
@@ -268,37 +268,33 @@ def tile_mistralattention_kernel(
         combine(2)
         store(2)
         multiply(3, (0,))
-        transposes(5, ALL)
-        evacuate(5, ALL, ())
-        quantise(4, WHOLE)
-        multiply(3, (1,))
-        transposes(6, (0, 1))
-        evacuate(6, (0, 1), ())
-        finish(3)
-        store(3)
-        quantise(5, WHOLE)
-        multiply(4, (0,))
-        transposes(6, (2, 3))
-        evacuate(6, (2, 3), ())
-        multiply(4, (1,))
-        for m in range(5, 14):
-            if m + 2 <= 13:
-                transposes(m + 2, (0,))
-                evacuate(m + 2, (0,), ())
-            if m == 12:
+
+        bank_list = [(n, g) for n in range(5, 14) for g in range(4)]
+        group_list = [(3, 1, 0), (3, 1, 1)] + [
+            (n, b, e) for n in range(4, 14) for b in range(2) for e in range(2)
+        ]
+        group_runs = (2, 2) + (3,) * 10 + (8,)
+
+        def after_unit(n):
+            if n == 11:
                 quantise(13, WHOLE)
-            finish(m - 1)
-            if m - 1 != 11:
-                store(m - 1)
-            if m - 1 == 12:
+            finish(n)
+            if n != 11:
+                store(n)
+            if n == 12:
                 store(11)
-            if m + 1 <= 12:
-                quantise(m + 1, WHOLE)
-            multiply_groups(m, 0, (0,))
-            for i in (1, 2, 3):
-                if m + 2 <= 13:
-                    transposes(m + 2, (i,))
-                    evacuate(m + 2, (i,), ())
-                multiply_groups(m, i // 2, (i % 2,))
-        finish(13)
-        store(13)
+            if 4 <= n <= 10:
+                quantise(n + 2, WHOLE)
+
+        first = 0
+        for r, size in enumerate(group_runs):
+            for n, g in bank_list[3 * r : 3 * r + 3]:
+                transposes(n, (g,))
+                evacuate(n, (g,), ())
+            if r < 2:
+                quantise(4 + r, WHOLE)
+            for n, b, e in group_list[first : first + size]:
+                multiply_groups(n, b, (e,))
+                if b == 1 and e == 1:
+                    after_unit(n)
+            first += size

from contextlib import ExitStack

import concourse.mybir as mybir
from concourse.masks import make_identity

FLOPS = 2 * 512 * 3072 * 2048

BF16 = mybir.dt.bfloat16
F32 = mybir.dt.float32
U32 = mybir.dt.uint32
U8 = mybir.dt.uint8
FP8X4 = mybir.dt.float8_e4m3fn_x4
MULT = mybir.AluOpType.mult
ADD = mybir.AluOpType.add

P = 128
LOAD_ORDER = (0, 2, 1, 3, 4, 5, 6, 7, 8, 9, 10, 11, 12, 13)
HALVED = (0, 1, 2, 3)
VECTOR_ADDS = (2, 3, 11)
FIRST_V_UNIT = 12


def tile_mistralattention_kernel(
    tc, hidden_states, cos, sin, q_w, k_w, v_w, out_0, out_1, out_2
):
    nc = tc.nc
    with ExitStack() as ctx:
        src_pool = ctx.enter_context(tc.tile_pool(name="src", bufs=1))
        const_pool = ctx.enter_context(tc.tile_pool(name="const", bufs=1))
        grp_pool = ctx.enter_context(tc.tile_pool(name="grp", bufs=3))
        xq_pool = ctx.enter_context(tc.tile_pool(name="xq", bufs=1))
        wq_pool = ctx.enter_context(tc.tile_pool(name="wq", bufs=3))
        tt_pool = ctx.enter_context(tc.tile_pool(name="tt", bufs=3))
        out_pool = ctx.enter_context(tc.tile_pool(name="outp", bufs=7))
        tp_pool = ctx.enter_context(tc.psum_pool(name="tp", bufs=4))
        acc_pool = ctx.enter_context(tc.psum_pool(name="acc", bufs=4))
        ctx.enter_context(tc.manual_schedule())

        def unit_rows(h):
            if h < 2:
                return hidden_states[h].rearrange("(p e) k -> p e k", e=2)
            w = h - 2
            if w < 8:
                rows = q_w[256 * w : 256 * w + 256, :]
            elif w < 10:
                rows = k_w[256 * (w - 8) : 256 * (w - 8) + 256, :]
            else:
                rows = v_w[256 * (w - 10) : 256 * (w - 10) + 256, :]
            return rows.rearrange("(r p) k -> p r k", p=P)

        def unit_out(h, b):
            w = h - 2
            if w < 8:
                dst = out_0[b, 2 * w : 2 * w + 2]
            elif w < 10:
                dst = out_1[b, 2 * (w - 8) : 2 * (w - 8) + 2]
            else:
                dst = out_2[b, 2 * (w - 10) : 2 * (w - 10) + 2]
            return dst.rearrange("h (p e) d -> p h (e d)", e=2)

        ident = const_pool.tile([P, P], F32, name="ident")
        make_identity(nc, ident[:])
        cos_sb = const_pool.tile([P, 512], BF16, name="cos_sb")
        sin_sb = const_pool.tile([P, 512], BF16, name="sin_sb")

        src = {}
        for h in LOAD_ORDER:
            rows = unit_rows(h)
            if h in HALVED:
                for i in range(2):
                    s_t = src_pool.tile([P, 2048], BF16, name="src%d_%d" % (h, i))
                    src[(h, i)] = s_t
                    nc.sync.dma_start(
                        out=s_t[:].rearrange("p (r k) -> p r k", r=2),
                        in_=rows[:, :, 1024 * i : 1024 * i + 1024],
                    )
            else:
                s_t = src_pool.tile([P, 4096], BF16, name="src%d" % h)
                src[(h, 0)] = s_t
                nc.sync.dma_start(out=s_t[:].rearrange("p (r k) -> p r k", r=2), in_=rows)
            if h == 3:
                nc.sync.dma_start(
                    out=cos_sb[:].rearrange("p (b x) -> p b x", b=2),
                    in_=cos.rearrange("b (p e) d -> p b (e d)", e=2),
                )
                nc.sync.dma_start(
                    out=sin_sb[:].rearrange("p (b x) -> p b x", b=2),
                    in_=sin.rearrange("b (p e) d -> p b (e d)", e=2),
                )

        def src_words(h, g, u, r):
            if h in HALVED:
                s_f = src[(h, g // 2)][:].bitcast(F32)
                col = 512 * r + 256 * (g % 2) + 128 * u
            else:
                s_f = src[(h, 0)][:].bitcast(F32)
                col = 1024 * r + 256 * g + 128 * u
            return s_f[:, col : col + 128]

        tab = const_pool.tile([P, 2048], F32, name="tab")
        tab_w = tab[:].rearrange("p (a t h c j) -> p a t h c j", a=2, t=4, h=2, c=2)
        tab_r = tab[:].rearrange("p (a b q c j) -> p a b q c j", a=2, b=2, q=4, c=2)
        cos_v = cos_sb[:].rearrange("p (t f j) -> p t f j", t=4, f=2)
        sin_v = sin_sb[:].rearrange("p (t f j) -> p t f j", t=4, f=2)

        def build_tables():
            for eng, a, c, view, f, sign in (
                (nc.vector, 0, 0, cos_v, 0, 1.0),
                (nc.gpsimd, 0, 1, sin_v, 1, 1.0),
                (nc.vector, 1, 0, cos_v, 1, 1.0),
                (nc.gpsimd, 1, 1, sin_v, 0, -1.0),
            ):
                eng.tensor_scalar(
                    out=tab_w[:, a, :, :, c, :],
                    in0=view[:, :, f, :].unsqueeze(2).to_broadcast([P, 4, 2, 64]),
                    scalar1=sign,
                    scalar2=0.0,
                    op0=MULT,
                    op1=ADD,
                )

        grouped = {}
        codes = {}
        planes = {}
        banks = {}
        sums = {}

        def transposes(h, gs):
            if h not in grouped:
                grouped[h] = grp_pool.tile([P, 4096], BF16, name="grp", align_bytes=64)
            for g in gs:
                pt = tp_pool.tile([P, 512], F32, name="pt")
                banks[(h, g)] = pt
                for u in range(2):
                    for r in range(2):
                        nc.tensor.transpose(
                            pt[:, 256 * u + 128 * r : 256 * u + 128 * r + 128],
                            src_words(h, g, u, r),
                            ident[:],
                        )

        def evacuate(h, gs, vector_gs):
            g_f = grouped[h][:].bitcast(F32)
            for g in gs:
                dst = g_f[:, 512 * g : 512 * g + 512].rearrange("p (o u) -> p o u", u=2)
                view = banks[(h, g)][:].rearrange("p (u o) -> p o u", u=2)
                if g in vector_gs:
                    nc.vector.tensor_copy(out=dst, in_=view)
                else:
                    nc.scalar.copy(out=dst, in_=view)

        def quantise(h, parts):
            if h not in codes:
                pool = xq_pool if h < 2 else wq_pool
                tag = "x%d" % h if h < 2 else "w"
                codes[h] = pool.tile([P, 1024], U32, name="codes_" + tag, align_bytes=64)
                planes[h] = pool.tile([P, 1024], U8, name="plane_" + tag, align_bytes=64)
            for lo, hi in parts:
                nc.vector.quantize_mx(
                    out=codes[h][:, lo:hi].bitcast(FP8X4),
                    scales=planes[h][:, lo:hi],
                    in_=grouped[h][:, 4 * lo : 4 * hi],
                )

        WHOLE = ((0, 1024),)

        def head_half(h, i):
            gs = (2 * i, 2 * i + 1)
            transposes(h, gs)
            evacuate(h, gs, (2 * i + 1,))
            quantise(h, ((512 * i, 512 * i + 512),))

        def multiply(h, bs):
            for b in bs:
                multiply_groups(h, b, (0, 1))

        def multiply_groups(h, b, es):
            if True:
                if (h, b) not in sums:
                    sums[(h, b)] = acc_pool.tile([P, 512], F32, name="acc")
                acc = sums[(h, b)]
                for e in es:
                    for g in range(4):
                        xs = slice(256 * g + 128 * e, 256 * g + 128 * e + 128)
                        ws = slice(256 * g, 256 * g + 256)
                        nc.tensor.matmul_mx(
                            out=acc[:, 256 * e : 256 * e + 256],
                            lhsT=codes[b][:, xs].bitcast(FP8X4),
                            lhsT_scale=planes[b][:, xs],
                            rhs=codes[h][:, ws].bitcast(FP8X4),
                            rhs_scale=planes[h][:, ws],
                            start=(g == 0),
                            stop=(g == 3),
                        )

        results = {}

        def store(h):
            o_b = results[h][:].rearrange("p (h b x) -> p h b x", h=2, b=2)
            for b in range(2):
                nc.sync.dma_start(out=unit_out(h, b), in_=o_b[:, :, b, :])

        terms = {}

        def products(h, b):
            if h not in results:
                results[h] = out_pool.tile([P, 1024], F32, name="o_t")
            if h >= FIRST_V_UNIT:
                o_v = results[h][:].rearrange("p (h t d) -> p t h d", h=2, t=4)
                nc.scalar.copy(
                    out=o_v[:, 2 * b : 2 * b + 2],
                    in_=sums[(h, b)][:].rearrange("p (e h d) -> p e h d", e=2, h=2),
                )
                return
            if h not in terms:
                terms[h] = tt_pool.tile([P, 2048], F32, name="t_t")
            tt5 = terms[h][:].rearrange("p (b q s j) -> p b q s j", b=2, q=4, s=4)
            acc4 = sums[(h, b)][:].rearrange("p (q f j) -> p q f j", q=4, f=2)
            nc.vector.tensor_tensor(
                out=tt5[:, b, :, 0:4:3, :],
                in0=acc4[:, :, 0:1, :].to_broadcast([P, 4, 2, 64]),
                in1=tab_r[:, 0, b],
                op=MULT,
            )
            nc.vector.tensor_tensor(
                out=tt5[:, b, :, 1:3, :],
                in0=acc4[:, :, 1:2, :].to_broadcast([P, 4, 2, 64]),
                in1=tab_r[:, 1, b],
                op=MULT,
            )

        def combine(h):
            if h >= FIRST_V_UNIT:
                return
            o_v = results[h][:].rearrange("p (h t d) -> p t h d", h=2, t=4)
            tt_u = terms[h][:].rearrange("p (t h s j) -> p t h s j", t=4, h=2, s=4)
            eng = nc.vector if h in VECTOR_ADDS else nc.gpsimd
            eng.tensor_tensor(
                out=o_v,
                in0=tt_u[:, :, :, 0:2, :].rearrange("p t h f j -> p t h (f j)"),
                in1=tt_u[:, :, :, 2:4, :].rearrange("p t h f j -> p t h (f j)"),
                op=ADD,
            )

        def finish(h):
            products(h, 0)
            products(h, 1)
            combine(h)

        ALL = (0, 1, 2, 3)

        for h in (0, 2, 1):
            head_half(h, 0)
            head_half(h, 1)
        multiply(2, (0,))
        transposes(3, (0, 1))
        evacuate(3, (0, 1), (1,))
        build_tables()
        quantise(3, ((0, 512),))
        multiply(2, (1,))
        transposes(3, (2, 3))
        evacuate(3, (2, 3), ())
        products(2, 0)
        quantise(3, ((512, 1024),))
        transposes(4, ALL)
        evacuate(4, ALL, ())
        products(2, 1)
        combine(2)
        store(2)
        multiply(3, (0,))

        bank_list = [(n, g) for n in range(5, 14) for g in range(4)]
        group_list = [(3, 1, 0), (3, 1, 1)] + [
            (n, b, e) for n in range(4, 14) for b in range(2) for e in range(2)
        ]
        group_runs = (2, 2) + (3,) * 10 + (8,)

        def after_unit(n):
            if n == 11:
                quantise(13, WHOLE)
            finish(n)
            if n != 11:
                store(n)
            if n == 12:
                store(11)
            if 4 <= n <= 10:
                quantise(n + 2, WHOLE)

        first = 0
        for r, size in enumerate(group_runs):
            for n, g in bank_list[3 * r : 3 * r + 3]:
                transposes(n, (g,))
                evacuate(n, (g,), ())
            if r < 2:
                quantise(4 + r, WHOLE)
            for n, b, e in group_list[first : first + size]:
                multiply_groups(n, b, (e,))
                if b == 1 and e == 1:
                    after_unit(n)
            first += size
